import numpy as np
import ml_dtypes


def mxq(x, axis, fmt="e4m3"):
    dtype, down = {"e4m3": (ml_dtypes.float8_e4m3fn, 7), "e5m2": (ml_dtypes.float8_e5m2, 14)}[fmt]
    v = np.moveaxis(np.asarray(x, np.float32).astype(ml_dtypes.bfloat16).astype(np.float64), axis, -1)
    blocks = v.reshape(v.shape[:-1] + (-1, 32))
    amax = np.abs(blocks).max(-1, keepdims=True)
    byte = np.maximum(np.where(amax > 0, np.frexp(amax)[1] - 1 + 127, 0) - down, 1)
    scale = np.exp2(byte - 127.0)
    codes = (blocks / scale).astype(np.float32).astype(dtype).astype(np.float64)
    return np.moveaxis((codes * scale).reshape(v.shape), -1, axis)


WIDE = False


def mx_kscale(k):
    if not WIDE:
        return np.ones(k)
    levels = np.array([10, -10, 5, -5, 0])
    a = np.random.permutation(np.resize(levels, k // 512 * 4)).reshape(k // 512, 4)
    idx = np.arange(k)
    return np.exp2(a[idx // 512, idx % 128 // 32])


BF16 = ml_dtypes.bfloat16


def bf(x):
    return np.asarray(x, np.float32).astype(BF16)


def f64(x):
    return np.asarray(x).astype(np.float64)


M, K, N, D = 1536, 1536, 1536, 128
GAMMA, ALPHA = 0.5, 0.1


def setup_inputs():
    s, t = mx_kscale(K), mx_kscale(N)
    return {"support0": bf(np.random.standard_normal((M, K)) / np.sqrt(K) * s),
            "f": bf(1.0 + 0.1 * np.random.standard_normal(K)),
            "support1": bf(np.random.standard_normal((K, N)) / np.sqrt(N) / s[:, None] * t),
            "adj": bf(np.random.standard_normal((M, N)) / np.sqrt(N) * t),
            "x": bf(np.random.standard_normal((N, D)) / t[:, None]),
            "h0": bf(np.random.standard_normal((M, D)))}


def reference(support0, f, support1, adj, x, h0):
    a = f64(support0) * f64(f)[None, :]
    bala2 = mxq(a, 1, "e4m3") @ mxq(f64(support1), 0, "e4m3")
    bala3 = GAMMA * bala2 + (1.0 - GAMMA) * f64(adj)
    hi = mxq(bala3, 1, "e4m3") @ mxq(f64(x), 0, "e4m3")
    return (1.0 - ALPHA) * hi + ALPHA * f64(h0)

@@ -1,0 +1,306 @@
+from contextlib import ExitStack
+
+import concourse.mybir as mybir
+from concourse.masks import make_identity
+
+F32 = mybir.dt.float32
+BF16 = mybir.dt.bfloat16
+U32 = mybir.dt.uint32
+U8 = mybir.dt.uint8
+FP8X4 = mybir.dt.float8_e4m3fn_x4
+ADD = mybir.AluOpType.add
+MULT = mybir.AluOpType.mult
+COPY = mybir.ActivationFunctionType.Copy
+
+P = 128
+SIZE = 1536
+D = 128
+PASS = 512
+HALF = 256
+N_PASS = SIZE // PASS
+THIRD = 512
+N_THIRD = SIZE // THIRD
+PAIR = 256
+N_PAIR = SIZE // PAIR
+ADJ_BUFS = 4
+
+GAMMA = 0.5
+ALPHA = 0.1
+
+FLOPS = 2 * SIZE * SIZE * SIZE + 2 * SIZE * SIZE * D
+
+
+def tile_combinelayer_pa_kernel(tc, support0, f, support1, adj, x, h0, out):
+    nc = tc.nc
+    with ExitStack() as ctx:
+        const = ctx.enter_context(tc.tile_pool(name="const", bufs=1))
+        keep = ctx.enter_context(tc.tile_pool(name="keep", bufs=1))
+        raw = ctx.enter_context(tc.tile_pool(name="raw", bufs=2))
+        stage = ctx.enter_context(tc.tile_pool(name="stage", bufs=4))
+        turned = ctx.enter_context(tc.psum_pool(name="turned", bufs=4))
+        sums = ctx.enter_context(tc.psum_pool(name="sums", bufs=3))
+        result = ctx.enter_context(tc.psum_pool(name="result", bufs=1))
+
+        ident = const.tile([P, P], F32, name="ident")
+        make_identity(nc, ident[:])
+
+
+        f_word = const.tile([P, N_PASS * 4], BF16, name="f_word")
+        nc.scalar.dma_start(
+            out=f_word[:].rearrange("q (h e) -> q h e", e=2),
+            in_=f.rearrange("(h q e) -> q h e", q=P, e=2),
+        )
+
+        s0_rows = []
+
+        def load_support0(pair):
+            rows = keep.tile([P, 2 * SIZE], BF16, name="s0_rows%d" % pair)
+            nc.sync.dma_start(
+                out=rows[:].rearrange("p (j k) -> p j k", j=2),
+                in_=support0[pair * PAIR : (pair + 1) * PAIR, :].rearrange("(j p) k -> p j k", p=P),
+            )
+            s0_rows.append(rows)
+
+        s1_rows = {}
+
+        def load_support1(block):
+            rows = raw.tile([P, N_PASS * 4 * PASS], BF16, name="s1_rows", tag="s1_rows")
+            view = rows[:].rearrange("q (h e n) -> q h e n", e=2, n=PASS)
+            for h in range(2 * N_PASS):
+                nc.sync.dma_start(
+                    out=view[:, h, :, :],
+                    in_=support1[
+                        h * HALF : (h + 1) * HALF, block * PASS : (block + 1) * PASS
+                    ].rearrange("(q e) n -> q e n", e=2),
+                )
+            s1_rows[block] = rows
+
+        adj_rows = {}
+
+        def load_adj(block, third):
+            rows = raw.tile([P, 4 * PASS], BF16, name="adj_rows", tag="adj_rows", bufs=ADJ_BUFS)
+            nc.sync.dma_start(
+                out=rows[:].rearrange("p (j n) -> p j n", j=4),
+                in_=adj[
+                    third * THIRD : (third + 1) * THIRD, block * PASS : (block + 1) * PASS
+                ].rearrange("(j p) n -> p j n", p=P),
+            )
+            adj_rows[(block, third)] = rows
+
+        s1_codes = {}
+        s1_scales = {}
+
+        def prepare_support1(block):
+            codes = keep.tile([P, N_PASS * PASS], U32, name="s1_codes%d" % block, align_bytes=64)
+            scales = keep.tile([P, N_PASS * PASS], U8, name="s1_scales%d" % block, align_bytes=64)
+            rows = s1_rows[block][:].rearrange("q (c t w e) -> q c e w t", c=N_PASS, t=4, e=2)
+            for c in range(N_PASS):
+                grouped = stage.tile([P, 4 * PASS], BF16, name="s1_grouped", tag="s1_grouped", bufs=3, align_bytes=64)
+                view = grouped[:].rearrange("q (e w t) -> q e w t", e=2, t=4)
+                if block == 0 and c > 0:
+                    nc.vector.tensor_copy(out=view, in_=rows[:, c])
+                else:
+                    nc.scalar.copy(out=view, in_=rows[:, c])
+                nc.vector.quantize_mx(
+                    out=codes[:, c * PASS : (c + 1) * PASS].bitcast(FP8X4),
+                    scales=scales[:, c * PASS : (c + 1) * PASS],
+                    in_=grouped[:],
+                )
+            s1_codes[block] = codes
+            s1_scales[block] = scales
+
+        a_codes = {}
+        a_scales = {}
+
+        def prepare_a(pair):
+            codes = keep.tile([P, N_PASS * PAIR], U32, name="a_codes%d" % pair, align_bytes=64)
+            scales = keep.tile([P, N_PASS * PAIR], U8, name="a_scales%d" % pair, align_bytes=64)
+            words = s0_rows[pair][:].bitcast(F32).rearrange("p (j w) -> p j w", j=2)
+            for c in range(N_PASS):
+                bank = turned.tile([P, 2 * PAIR], F32, name="a_bank", tag="turned")
+                for u in range(2):
+                    for j in range(2):
+                        nc.tensor.transpose(
+                            bank[:, u * PAIR + j * P : u * PAIR + (j + 1) * P],
+                            words[:, j, (2 * c + u) * P : (2 * c + u + 1) * P],
+                            ident[:],
+                        )
+                grouped = stage.tile([P, 4 * PAIR], BF16, name="a_grouped", tag="a_grouped", align_bytes=64)
+                nc.vector.tensor_tensor(
+                    out=grouped[:].rearrange("q (m u e) -> q m u e", u=2, e=2),
+                    in0=bank[:].bitcast(BF16).rearrange("q (u m e) -> q m u e", u=2, e=2),
+                    in1=f_word[:, 4 * c : 4 * c + 4]
+                    .rearrange("q (u e) -> q u e", e=2)
+                    .unsqueeze(1)
+                    .to_broadcast([P, PAIR, 2, 2]),
+                    op=MULT,
+                )
+                nc.vector.quantize_mx(
+                    out=codes[:, c * PAIR : (c + 1) * PAIR].bitcast(FP8X4),
+                    scales=scales[:, c * PAIR : (c + 1) * PAIR],
+                    in_=grouped[:],
+                )
+            a_codes[pair] = codes
+            a_scales[pair] = scales
+
+        adj_half = {}
+
+        def prepare_adj(block, third):
+            words = adj_rows[(block, third)][:].bitcast(F32).rearrange("p (j w) -> p j w", j=4)
+            for i in range(2):
+                bank = turned.tile([P, 2 * PAIR], F32, name="adj_bank", tag="turned")
+                for u in range(2):
+                    for j in range(2):
+                        nc.tensor.transpose(
+                            bank[:, u * PAIR + j * P : u * PAIR + (j + 1) * P],
+                            words[:, 2 * i + j, u * P : (u + 1) * P],
+                            ident[:],
+                        )
+                half = stage.tile([P, 4 * PAIR], BF16, name="adj_half", tag="adj_half", bufs=6)
+                nc.scalar.activation(
+                    out=half[:].rearrange("q (m u e) -> q m u e", u=2, e=2),
+                    in_=bank[:].bitcast(BF16).rearrange("q (u m e) -> q m u e", u=2, e=2),
+                    func=COPY,
+                    scale=1.0 - GAMMA,
+                )
+                adj_half[(block, 2 * third + i)] = half
+
+        g_codes = []
+        g_scales = []
+        for pair in range(N_PAIR):
+            g_codes.append(keep.tile([P, N_PASS * PAIR], U32, name="g_codes%d" % pair, align_bytes=64))
+            g_scales.append(keep.tile([P, N_PASS * PAIR], U8, name="g_scales%d" % pair, align_bytes=64))
+
+        def first_matmul(block, pair):
+            grouped = stage.tile([P, 4 * PAIR], BF16, name="g_grouped", tag="g_grouped", align_bytes=64)
+            for j in range(2):
+                bank = sums.tile([P, 4 * P], F32, name="p_bank", tag="sums")
+                for u in range(2):
+                    for e in range(2):
+                        t = 2 * u + e
+                        for c in range(N_PASS):
+                            cols = slice(c * PASS + e * HALF + u * P, c * PASS + e * HALF + (u + 1) * P)
+                            rows = slice(c * PAIR + j * P, c * PAIR + (j + 1) * P)
+                            nc.tensor.matmul_mx(
+                                out=bank[:, t * P : (t + 1) * P],
+                                lhsT=s1_codes[block][:, cols].bitcast(FP8X4),
+                                lhsT_scale=s1_scales[block][:, cols],
+                                rhs=a_codes[pair][:, rows].bitcast(FP8X4),
+                                rhs_scale=a_scales[pair][:, rows],
+                                start=(c == 0),
+                                stop=(c == N_PASS - 1),
+                            )
+                nc.vector.scalar_tensor_tensor(
+                    out=grouped[:, j * 4 * P : (j + 1) * 4 * P],
+                    in0=bank[:].rearrange("q (t m) -> q m t", t=4),
+                    scalar=GAMMA,
+                    in1=adj_half[(block, pair)][:, j * 4 * P : (j + 1) * 4 * P],
+                    op0=MULT,
+                    op1=ADD,
+                )
+            nc.vector.quantize_mx(
+                out=g_codes[pair][:, block * PAIR : (block + 1) * PAIR].bitcast(FP8X4),
+                scales=g_scales[pair][:, block * PAIR : (block + 1) * PAIR],
+                in_=grouped[:],
+            )
+
+        x_codes = keep.tile([P, N_PASS * D], U32, name="x_codes", align_bytes=64)
+        x_scales = keep.tile([P, N_PASS * D], U8, name="x_scales", align_bytes=64)
+        x_rows = keep.tile([P, N_PASS * 4 * D], BF16, name="x_rows")
+        h0_rows = keep.tile([P, (SIZE // P) * D], BF16, name="h0_rows")
+        h0_part = keep.tile([P, (SIZE // P) * D], F32, name="h0_part")
+
+        def load_x_h0():
+            nc.sync.dma_start(
+                out=x_rows[:].rearrange("q (h e d) -> q h e d", e=2, d=D),
+                in_=x.rearrange("(h q e) d -> q h e d", q=P, e=2),
+            )
+            nc.sync.dma_start(
+                out=h0_rows[:].rearrange("p (j d) -> p j d", d=D),
+                in_=h0.rearrange("(j p) d -> p j d", p=P),
+            )
+
+        def prepare_x_h0():
+            grouped = keep.tile([P, N_PASS * 4 * D], BF16, name="x_grouped", align_bytes=64)
+            nc.scalar.copy(
+                out=grouped[:].rearrange("q (c d t) -> q c d t", c=N_PASS, t=4),
+                in_=x_rows[:].rearrange("q (c t d) -> q c d t", c=N_PASS, t=4),
+            )
+            nc.scalar.activation(out=h0_part[:], in_=h0_rows[:], func=COPY, scale=ALPHA)
+            for c in range(N_PASS):
+                nc.vector.quantize_mx(
+                    out=x_codes[:, c * D : (c + 1) * D].bitcast(FP8X4),
+                    scales=x_scales[:, c * D : (c + 1) * D],
+                    in_=grouped[:, c * 4 * D : (c + 1) * 4 * D],
+                )
+
+        def second_matmul(third):
+            bank = result.tile([P, 4 * D], F32, name="hi_bank", tag="result")
+            for i in range(4):
+                pair = 2 * third + i // 2
+                j = i % 2
+                for c in range(N_PASS):
+                    cols = slice(c * PAIR + j * P, c * PAIR + (j + 1) * P)
+                    nc.tensor.matmul_mx(
+                        out=bank[:, i * D : (i + 1) * D],
+                        lhsT=g_codes[pair][:, cols].bitcast(FP8X4),
+                        lhsT_scale=g_scales[pair][:, cols],
+                        rhs=x_codes[:, c * D : (c + 1) * D].bitcast(FP8X4),
+                        rhs_scale=x_scales[:, c * D : (c + 1) * D],
+                        start=(c == 0),
+                        stop=(c == N_PASS - 1),
+                    )
+            rows = stage.tile([P, 4 * D], F32, name="out_rows", tag="out_rows", bufs=2)
+            nc.vector.scalar_tensor_tensor(
+                out=rows[:],
+                in0=bank[:],
+                scalar=1.0 - ALPHA,
+                in1=h0_part[:, third * 4 * D : (third + 1) * 4 * D],
+                op0=MULT,
+                op1=ADD,
+            )
+            nc.sync.dma_start(
+                out=out[third * THIRD : (third + 1) * THIRD, :].rearrange("(j p) d -> p j d", p=P),
+                in_=rows[:].rearrange("p (j d) -> p j d", d=D),
+            )
+
+        steps = [(block, third) for block in range(N_PASS) for third in range(N_THIRD)]
+
+        def prepare(i):
+            block, third = steps[i]
+            if third == 0:
+                prepare_support1(block)
+                if block + 2 < N_PASS:
+                    load_support1(block + 2)
+            if block == 0:
+                prepare_a(2 * third)
+                prepare_a(2 * third + 1)
+            prepare_adj(block, third)
+            if i + ADJ_BUFS < len(steps):
+                load_adj(*steps[i + ADJ_BUFS])
+
+        load_support0(0)
+        load_support1(0)
+        load_adj(*steps[0])
+        load_support0(1)
+        load_support0(2)
+        load_support0(3)
+        load_adj(*steps[1])
+        load_support0(4)
+        load_support0(5)
+        load_adj(*steps[2])
+        load_support1(1)
+        load_adj(*steps[3])
+        load_x_h0()
+
+        prepare(0)
+        for i in range(len(steps)):
+            block, third = steps[i]
+            if i + 1 < len(steps):
+                prepare(i + 1)
+            if block == N_PASS - 1 and third == 0:
+                prepare_x_h0()
+            first_matmul(block, 2 * third)
+            first_matmul(block, 2 * third + 1)
+            if block == N_PASS - 1:
+                second_matmul(third)

@@ -18,11 +18,11 @@ D = 128
 PASS = 512
 HALF = 256
 N_PASS = SIZE // PASS
-THIRD = 512
-N_THIRD = SIZE // THIRD
 PAIR = 256
 N_PAIR = SIZE // PAIR
-ADJ_BUFS = 4
+N_STEP = N_PASS * N_PAIR
+REGROUP_FROM = 3
+SECOND_LAG = 2
 
 GAMMA = 0.5
 ALPHA = 0.1
@@ -35,7 +35,6 @@ def tile_combinelayer_pa_kernel(tc, support0, f, support1, adj, x, h0, out):
     with ExitStack() as ctx:
         const = ctx.enter_context(tc.tile_pool(name="const", bufs=1))
         keep = ctx.enter_context(tc.tile_pool(name="keep", bufs=1))
-        raw = ctx.enter_context(tc.tile_pool(name="raw", bufs=2))
         stage = ctx.enter_context(tc.tile_pool(name="stage", bufs=4))
         turned = ctx.enter_context(tc.psum_pool(name="turned", bufs=4))
         sums = ctx.enter_context(tc.psum_pool(name="sums", bufs=3))
@@ -44,14 +43,20 @@ def tile_combinelayer_pa_kernel(tc, support0, f, support1, adj, x, h0, out):
         ident = const.tile([P, P], F32, name="ident")
         make_identity(nc, ident[:])
 
+        ctx.enter_context(tc.manual_schedule())
+
 
         f_word = const.tile([P, N_PASS * 4], BF16, name="f_word")
         nc.scalar.dma_start(
             out=f_word[:].rearrange("q (h e) -> q h e", e=2),
             in_=f.rearrange("(h q e) -> q h e", q=P, e=2),
         )
+        warm = const.tile([P, 1], F32, name="warm")
+        nc.scalar.activation(out=warm[:], in_=ident[:, 0:1], func=COPY, scale=1.0)
 
-        s0_rows = []
+        s0_rows = {}
+        s1_rows = {}
+        adj_rows = {}
 
         def load_support0(pair):
             rows = keep.tile([P, 2 * SIZE], BF16, name="s0_rows%d" % pair)
@@ -59,12 +64,10 @@ def tile_combinelayer_pa_kernel(tc, support0, f, support1, adj, x, h0, out):
                 out=rows[:].rearrange("p (j k) -> p j k", j=2),
                 in_=support0[pair * PAIR : (pair + 1) * PAIR, :].rearrange("(j p) k -> p j k", p=P),
             )
-            s0_rows.append(rows)
-
-        s1_rows = {}
+            s0_rows[pair] = rows
 
         def load_support1(block):
-            rows = raw.tile([P, N_PASS * 4 * PASS], BF16, name="s1_rows", tag="s1_rows")
+            rows = keep.tile([P, N_PASS * 4 * PASS], BF16, name="s1_rows", tag="s1_rows", bufs=2)
             view = rows[:].rearrange("q (h e n) -> q h e n", e=2, n=PASS)
             for h in range(2 * N_PASS):
                 nc.sync.dma_start(
@@ -75,140 +78,18 @@ def tile_combinelayer_pa_kernel(tc, support0, f, support1, adj, x, h0, out):
                 )
             s1_rows[block] = rows
 
-        adj_rows = {}
-
-        def load_adj(block, third):
-            rows = raw.tile([P, 4 * PASS], BF16, name="adj_rows", tag="adj_rows", bufs=ADJ_BUFS)
+        def load_adj(block, pair):
+            rows = keep.tile([P, 2 * PASS], BF16, name="adj_rows%d_%d" % (block, pair))
             nc.sync.dma_start(
-                out=rows[:].rearrange("p (j n) -> p j n", j=4),
+                out=rows[:].rearrange("p (j n) -> p j n", j=2),
                 in_=adj[
-                    third * THIRD : (third + 1) * THIRD, block * PASS : (block + 1) * PASS
+                    pair * PAIR : (pair + 1) * PAIR, block * PASS : (block + 1) * PASS
                 ].rearrange("(j p) n -> p j n", p=P),
             )
-            adj_rows[(block, third)] = rows
+            adj_rows[(block, pair)] = rows
 
-        s1_codes = {}
-        s1_scales = {}
-
-        def prepare_support1(block):
-            codes = keep.tile([P, N_PASS * PASS], U32, name="s1_codes%d" % block, align_bytes=64)
-            scales = keep.tile([P, N_PASS * PASS], U8, name="s1_scales%d" % block, align_bytes=64)
-            rows = s1_rows[block][:].rearrange("q (c t w e) -> q c e w t", c=N_PASS, t=4, e=2)
-            for c in range(N_PASS):
-                grouped = stage.tile([P, 4 * PASS], BF16, name="s1_grouped", tag="s1_grouped", bufs=3, align_bytes=64)
-                view = grouped[:].rearrange("q (e w t) -> q e w t", e=2, t=4)
-                if block == 0 and c > 0:
-                    nc.vector.tensor_copy(out=view, in_=rows[:, c])
-                else:
-                    nc.scalar.copy(out=view, in_=rows[:, c])
-                nc.vector.quantize_mx(
-                    out=codes[:, c * PASS : (c + 1) * PASS].bitcast(FP8X4),
-                    scales=scales[:, c * PASS : (c + 1) * PASS],
-                    in_=grouped[:],
-                )
-            s1_codes[block] = codes
-            s1_scales[block] = scales
-
-        a_codes = {}
-        a_scales = {}
-
-        def prepare_a(pair):
-            codes = keep.tile([P, N_PASS * PAIR], U32, name="a_codes%d" % pair, align_bytes=64)
-            scales = keep.tile([P, N_PASS * PAIR], U8, name="a_scales%d" % pair, align_bytes=64)
-            words = s0_rows[pair][:].bitcast(F32).rearrange("p (j w) -> p j w", j=2)
-            for c in range(N_PASS):
-                bank = turned.tile([P, 2 * PAIR], F32, name="a_bank", tag="turned")
-                for u in range(2):
-                    for j in range(2):
-                        nc.tensor.transpose(
-                            bank[:, u * PAIR + j * P : u * PAIR + (j + 1) * P],
-                            words[:, j, (2 * c + u) * P : (2 * c + u + 1) * P],
-                            ident[:],
-                        )
-                grouped = stage.tile([P, 4 * PAIR], BF16, name="a_grouped", tag="a_grouped", align_bytes=64)
-                nc.vector.tensor_tensor(
-                    out=grouped[:].rearrange("q (m u e) -> q m u e", u=2, e=2),
-                    in0=bank[:].bitcast(BF16).rearrange("q (u m e) -> q m u e", u=2, e=2),
-                    in1=f_word[:, 4 * c : 4 * c + 4]
-                    .rearrange("q (u e) -> q u e", e=2)
-                    .unsqueeze(1)
-                    .to_broadcast([P, PAIR, 2, 2]),
-                    op=MULT,
-                )
-                nc.vector.quantize_mx(
-                    out=codes[:, c * PAIR : (c + 1) * PAIR].bitcast(FP8X4),
-                    scales=scales[:, c * PAIR : (c + 1) * PAIR],
-                    in_=grouped[:],
-                )
-            a_codes[pair] = codes
-            a_scales[pair] = scales
-
-        adj_half = {}
-
-        def prepare_adj(block, third):
-            words = adj_rows[(block, third)][:].bitcast(F32).rearrange("p (j w) -> p j w", j=4)
-            for i in range(2):
-                bank = turned.tile([P, 2 * PAIR], F32, name="adj_bank", tag="turned")
-                for u in range(2):
-                    for j in range(2):
-                        nc.tensor.transpose(
-                            bank[:, u * PAIR + j * P : u * PAIR + (j + 1) * P],
-                            words[:, 2 * i + j, u * P : (u + 1) * P],
-                            ident[:],
-                        )
-                half = stage.tile([P, 4 * PAIR], BF16, name="adj_half", tag="adj_half", bufs=6)
-                nc.scalar.activation(
-                    out=half[:].rearrange("q (m u e) -> q m u e", u=2, e=2),
-                    in_=bank[:].bitcast(BF16).rearrange("q (u m e) -> q m u e", u=2, e=2),
-                    func=COPY,
-                    scale=1.0 - GAMMA,
-                )
-                adj_half[(block, 2 * third + i)] = half
-
-        g_codes = []
-        g_scales = []
-        for pair in range(N_PAIR):
-            g_codes.append(keep.tile([P, N_PASS * PAIR], U32, name="g_codes%d" % pair, align_bytes=64))
-            g_scales.append(keep.tile([P, N_PASS * PAIR], U8, name="g_scales%d" % pair, align_bytes=64))
-
-        def first_matmul(block, pair):
-            grouped = stage.tile([P, 4 * PAIR], BF16, name="g_grouped", tag="g_grouped", align_bytes=64)
-            for j in range(2):
-                bank = sums.tile([P, 4 * P], F32, name="p_bank", tag="sums")
-                for u in range(2):
-                    for e in range(2):
-                        t = 2 * u + e
-                        for c in range(N_PASS):
-                            cols = slice(c * PASS + e * HALF + u * P, c * PASS + e * HALF + (u + 1) * P)
-                            rows = slice(c * PAIR + j * P, c * PAIR + (j + 1) * P)
-                            nc.tensor.matmul_mx(
-                                out=bank[:, t * P : (t + 1) * P],
-                                lhsT=s1_codes[block][:, cols].bitcast(FP8X4),
-                                lhsT_scale=s1_scales[block][:, cols],
-                                rhs=a_codes[pair][:, rows].bitcast(FP8X4),
-                                rhs_scale=a_scales[pair][:, rows],
-                                start=(c == 0),
-                                stop=(c == N_PASS - 1),
-                            )
-                nc.vector.scalar_tensor_tensor(
-                    out=grouped[:, j * 4 * P : (j + 1) * 4 * P],
-                    in0=bank[:].rearrange("q (t m) -> q m t", t=4),
-                    scalar=GAMMA,
-                    in1=adj_half[(block, pair)][:, j * 4 * P : (j + 1) * 4 * P],
-                    op0=MULT,
-                    op1=ADD,
-                )
-            nc.vector.quantize_mx(
-                out=g_codes[pair][:, block * PAIR : (block + 1) * PAIR].bitcast(FP8X4),
-                scales=g_scales[pair][:, block * PAIR : (block + 1) * PAIR],
-                in_=grouped[:],
-            )
-
-        x_codes = keep.tile([P, N_PASS * D], U32, name="x_codes", align_bytes=64)
-        x_scales = keep.tile([P, N_PASS * D], U8, name="x_scales", align_bytes=64)
         x_rows = keep.tile([P, N_PASS * 4 * D], BF16, name="x_rows")
         h0_rows = keep.tile([P, (SIZE // P) * D], BF16, name="h0_rows")
-        h0_part = keep.tile([P, (SIZE // P) * D], F32, name="h0_part")
 
         def load_x_h0():
             nc.sync.dma_start(
@@ -220,29 +101,167 @@ def tile_combinelayer_pa_kernel(tc, support0, f, support1, adj, x, h0, out):
                 in_=h0.rearrange("(j p) d -> p j d", p=P),
             )
 
-        def prepare_x_h0():
-            grouped = keep.tile([P, N_PASS * 4 * D], BF16, name="x_grouped", align_bytes=64)
+        s1_codes = {}
+        s1_scales = {}
+        s1_grouped = {}
+        for block in range(N_PASS):
+            s1_codes[block] = keep.tile([P, N_PASS * PASS], U32, name="s1_codes%d" % block, align_bytes=64)
+            s1_scales[block] = keep.tile([P, N_PASS * PASS], U8, name="s1_scales%d" % block, align_bytes=64)
+
+        def regroup_support1(block, c, on_vector):
+            rows = s1_rows[block][:].rearrange("q (c t w e) -> q c e w t", c=N_PASS, t=4, e=2)
+            grouped = stage.tile([P, 4 * PASS], BF16, name="s1_grouped", tag="s1_grouped", bufs=3, align_bytes=64)
+            view = grouped[:].rearrange("q (e w t) -> q e w t", e=2, t=4)
+            if on_vector:
+                nc.vector.tensor_copy(out=view, in_=rows[:, c])
+            else:
+                nc.scalar.copy(out=view, in_=rows[:, c])
+            s1_grouped[(block, c)] = grouped
+
+        def quantise_support1(block, c):
+            nc.vector.quantize_mx(
+                out=s1_codes[block][:, c * PASS : (c + 1) * PASS].bitcast(FP8X4),
+                scales=s1_scales[block][:, c * PASS : (c + 1) * PASS],
+                in_=s1_grouped[(block, c)][:],
+            )
+
+        a_codes = {}
+        a_scales = {}
+        a_grouped = {}
+        for pair in range(N_PAIR):
+            a_codes[pair] = keep.tile([P, N_PASS * PAIR], U32, name="a_codes%d" % pair, align_bytes=64)
+            a_scales[pair] = keep.tile([P, N_PASS * PAIR], U8, name="a_scales%d" % pair, align_bytes=64)
+
+        def turn_and_scale_support0(pair, c):
+            words = s0_rows[pair][:].bitcast(F32).rearrange("p (j w) -> p j w", j=2)
+            bank = turned.tile([P, 2 * PAIR], F32, name="a_bank", tag="turned")
+            for u in range(2):
+                for j in range(2):
+                    nc.tensor.transpose(
+                        bank[:, u * PAIR + j * P : u * PAIR + (j + 1) * P],
+                        words[:, j, (2 * c + u) * P : (2 * c + u + 1) * P],
+                        ident[:],
+                    )
+            grouped = stage.tile([P, 4 * PAIR], BF16, name="a_grouped", tag="a_grouped", align_bytes=64)
+            nc.vector.tensor_tensor(
+                out=grouped[:].rearrange("q (m u e) -> q m u e", u=2, e=2),
+                in0=bank[:].bitcast(BF16).rearrange("q (u m e) -> q m u e", u=2, e=2),
+                in1=f_word[:, 4 * c : 4 * c + 4]
+                .rearrange("q (u e) -> q u e", e=2)
+                .unsqueeze(1)
+                .to_broadcast([P, PAIR, 2, 2]),
+                op=MULT,
+            )
+            a_grouped[(pair, c)] = grouped
+
+        def quantise_a(pair, c):
+            nc.vector.quantize_mx(
+                out=a_codes[pair][:, c * PAIR : (c + 1) * PAIR].bitcast(FP8X4),
+                scales=a_scales[pair][:, c * PAIR : (c + 1) * PAIR],
+                in_=a_grouped[(pair, c)][:],
+            )
+
+        adj_half = {}
+
+        def turn_and_halve_adj(step):
+            block, pair = divmod(step, N_PAIR)
+            words = adj_rows[(block, pair)][:].bitcast(F32).rearrange("p (j w) -> p j w", j=2)
+            bank = turned.tile([P, 2 * PAIR], F32, name="adj_bank", tag="turned")
+            for u in range(2):
+                for j in range(2):
+                    nc.tensor.transpose(
+                        bank[:, u * PAIR + j * P : u * PAIR + (j + 1) * P],
+                        words[:, j, u * P : (u + 1) * P],
+                        ident[:],
+                    )
+            half = stage.tile([P, 4 * PAIR], BF16, name="adj_half", tag="adj_half")
+            nc.scalar.activation(
+                out=half[:].rearrange("q (m u e) -> q m u e", u=2, e=2),
+                in_=bank[:].bitcast(BF16).rearrange("q (u m e) -> q m u e", u=2, e=2),
+                func=COPY,
+                scale=1.0 - GAMMA,
+            )
+            adj_half[step] = half
+
+        g_codes = {}
+        g_scales = {}
+        g_grouped = {}
+        p_bank = {}
+        for pair in range(N_PAIR):
+            g_codes[pair] = keep.tile([P, N_PASS * PAIR], U32, name="g_codes%d" % pair, align_bytes=64)
+            g_scales[pair] = keep.tile([P, N_PASS * PAIR], U8, name="g_scales%d" % pair, align_bytes=64)
+
+        def first_matmul(step, j):
+            block, pair = divmod(step, N_PAIR)
+            bank = sums.tile([P, 4 * P], F32, name="p_bank", tag="sums")
+            for u in range(2):
+                for e in range(2):
+                    t = 2 * u + e
+                    for c in range(N_PASS):
+                        cols = slice(c * PASS + e * HALF + u * P, c * PASS + e * HALF + (u + 1) * P)
+                        rows = slice(c * PAIR + j * P, c * PAIR + (j + 1) * P)
+                        nc.tensor.matmul_mx(
+                            out=bank[:, t * P : (t + 1) * P],
+                            lhsT=s1_codes[block][:, cols].bitcast(FP8X4),
+                            lhsT_scale=s1_scales[block][:, cols],
+                            rhs=a_codes[pair][:, rows].bitcast(FP8X4),
+                            rhs_scale=a_scales[pair][:, rows],
+                            start=(c == 0),
+                            stop=(c == N_PASS - 1),
+                        )
+            p_bank[(step, j)] = bank
+
+        def blend(step, j):
+            if j == 0:
+                g_grouped[step] = stage.tile(
+                    [P, 4 * PAIR], BF16, name="g_grouped", tag="g_grouped", bufs=3, align_bytes=64
+                )
+            nc.vector.scalar_tensor_tensor(
+                out=g_grouped[step][:, j * 4 * P : (j + 1) * 4 * P],
+                in0=p_bank[(step, j)][:].rearrange("q (t m) -> q m t", t=4),
+                scalar=GAMMA,
+                in1=adj_half[step][:, j * 4 * P : (j + 1) * 4 * P],
+                op0=MULT,
+                op1=ADD,
+            )
+
+        def quantise_g(step):
+            block, pair = divmod(step, N_PAIR)
+            nc.vector.quantize_mx(
+                out=g_codes[pair][:, block * PAIR : (block + 1) * PAIR].bitcast(FP8X4),
+                scales=g_scales[pair][:, block * PAIR : (block + 1) * PAIR],
+                in_=g_grouped[step][:],
+            )
+
+        x_codes = keep.tile([P, N_PASS * D], U32, name="x_codes", align_bytes=64)
+        x_scales = keep.tile([P, N_PASS * D], U8, name="x_scales", align_bytes=64)
+        x_grouped = keep.tile([P, N_PASS * 4 * D], BF16, name="x_grouped", align_bytes=64)
+        h0_part = keep.tile([P, (SIZE // P) * D], F32, name="h0_part")
+
+        def regroup_x_scale_h0():
             nc.scalar.copy(
-                out=grouped[:].rearrange("q (c d t) -> q c d t", c=N_PASS, t=4),
+                out=x_grouped[:].rearrange("q (c d t) -> q c d t", c=N_PASS, t=4),
                 in_=x_rows[:].rearrange("q (c t d) -> q c d t", c=N_PASS, t=4),
             )
             nc.scalar.activation(out=h0_part[:], in_=h0_rows[:], func=COPY, scale=ALPHA)
+
+        def quantise_x():
             for c in range(N_PASS):
                 nc.vector.quantize_mx(
                     out=x_codes[:, c * D : (c + 1) * D].bitcast(FP8X4),
                     scales=x_scales[:, c * D : (c + 1) * D],
-                    in_=grouped[:, c * 4 * D : (c + 1) * 4 * D],
+                    in_=x_grouped[:, c * 4 * D : (c + 1) * 4 * D],
                 )
 
-        def second_matmul(third):
-            bank = result.tile([P, 4 * D], F32, name="hi_bank", tag="result")
-            for i in range(4):
-                pair = 2 * third + i // 2
-                j = i % 2
+        hi_bank = {}
+
+        def second_matmul(pair):
+            bank = result.tile([P, 2 * D], F32, name="hi_bank", tag="result")
+            for j in range(2):
                 for c in range(N_PASS):
                     cols = slice(c * PAIR + j * P, c * PAIR + (j + 1) * P)
                     nc.tensor.matmul_mx(
-                        out=bank[:, i * D : (i + 1) * D],
+                        out=bank[:, j * D : (j + 1) * D],
                         lhsT=g_codes[pair][:, cols].bitcast(FP8X4),
                         lhsT_scale=g_scales[pair][:, cols],
                         rhs=x_codes[:, c * D : (c + 1) * D].bitcast(FP8X4),
@@ -250,57 +269,101 @@ def tile_combinelayer_pa_kernel(tc, support0, f, support1, adj, x, h0, out):
                         start=(c == 0),
                         stop=(c == N_PASS - 1),
                     )
-            rows = stage.tile([P, 4 * D], F32, name="out_rows", tag="out_rows", bufs=2)
+            hi_bank[pair] = bank
+
+        def finish(pair):
+            rows = stage.tile([P, 2 * D], F32, name="out_rows", tag="out_rows", bufs=2)
             nc.vector.scalar_tensor_tensor(
                 out=rows[:],
-                in0=bank[:],
+                in0=hi_bank[pair][:],
                 scalar=1.0 - ALPHA,
-                in1=h0_part[:, third * 4 * D : (third + 1) * 4 * D],
+                in1=h0_part[:, pair * 2 * D : (pair + 1) * 2 * D],
                 op0=MULT,
                 op1=ADD,
             )
             nc.sync.dma_start(
-                out=out[third * THIRD : (third + 1) * THIRD, :].rearrange("(j p) d -> p j d", p=P),
+                out=out[pair * PAIR : (pair + 1) * PAIR, :].rearrange("(j p) d -> p j d", p=P),
                 in_=rows[:].rearrange("p (j d) -> p j d", d=D),
             )
 
-        steps = [(block, third) for block in range(N_PASS) for third in range(N_THIRD)]
-
-        def prepare(i):
-            block, third = steps[i]
-            if third == 0:
-                prepare_support1(block)
-                if block + 2 < N_PASS:
-                    load_support1(block + 2)
-            if block == 0:
-                prepare_a(2 * third)
-                prepare_a(2 * third + 1)
-            prepare_adj(block, third)
-            if i + ADJ_BUFS < len(steps):
-                load_adj(*steps[i + ADJ_BUFS])
-
         load_support0(0)
         load_support1(0)
-        load_adj(*steps[0])
-        load_support0(1)
-        load_support0(2)
-        load_support0(3)
-        load_adj(*steps[1])
-        load_support0(4)
-        load_support0(5)
-        load_adj(*steps[2])
-        load_support1(1)
-        load_adj(*steps[3])
-        load_x_h0()
+        load_adj(0, 0)
+        for pair in range(1, N_PAIR):
+            load_support0(pair)
+            load_adj(0, pair)
+            if pair == REGROUP_FROM:
+                load_support1(1)
+        for pair in range(N_PAIR):
+            load_adj(1, pair)
 
-        prepare(0)
-        for i in range(len(steps)):
-            block, third = steps[i]
-            if i + 1 < len(steps):
-                prepare(i + 1)
-            if block == N_PASS - 1 and third == 0:
-                prepare_x_h0()
-            first_matmul(block, 2 * third)
-            first_matmul(block, 2 * third + 1)
-            if block == N_PASS - 1:
-                second_matmul(third)
+        turn_and_scale_support0(0, 0)
+        turn_and_scale_support0(0, 1)
+        quantise_a(0, 0)
+        turn_and_scale_support0(0, 2)
+        quantise_a(0, 1)
+        regroup_support1(0, 0, False)
+        regroup_support1(0, 1, False)
+        quantise_a(0, 2)
+        regroup_support1(0, 2, True)
+        for c in range(N_PASS):
+            quantise_support1(0, c)
+        turn_and_halve_adj(0)
+
+        load_support1(2)
+        load_x_h0()
+        for pair in range(N_PAIR):
+            load_adj(2, pair)
+
+        for step in range(N_STEP):
+            block, pair = divmod(step, N_PAIR)
+            prepare = block == 0 and pair + 1 < N_PAIR
+
+            if prepare:
+                turn_and_scale_support0(pair + 1, 0)
+                turn_and_scale_support0(pair + 1, 1)
+                quantise_a(pair + 1, 0)
+                turn_and_scale_support0(pair + 1, 2)
+                quantise_a(pair + 1, 1)
+            if block == 0:
+                turn_and_halve_adj(step + 1)
+            elif step % 2 == 0:
+                for later in (step + 1, step + 2):
+                    if later < N_STEP:
+                        turn_and_halve_adj(later)
+            first_matmul(step, 0)
+            first_matmul(step, 1)
+            if block == N_PASS - 1 and pair >= SECOND_LAG:
+                second_matmul(pair - SECOND_LAG)
+
+            regroup = None
+            if block == 0 and pair >= REGROUP_FROM:
+                regroup = pair - REGROUP_FROM
+            if block == 1 and pair < N_PASS:
+                regroup = pair
+            if regroup is not None:
+                regroup_support1(block + 1, regroup, False)
+            if step == (N_PASS - 1) * N_PAIR:
+                regroup_x_scale_h0()
+
+            blend(step, 0)
+            if prepare:
+                quantise_a(pair + 1, 2)
+            if step > 0:
+                quantise_g(step - 1)
+            if regroup is not None and regroup > 0:
+                quantise_support1(block + 1, regroup - 1)
+            if block == 1 and pair == N_PASS:
+                quantise_support1(block + 1, N_PASS - 1)
+            blend(step, 1)
+            if block == 0 and pair == N_PAIR - 1:
+                quantise_support1(block + 1, N_PASS - 1)
+            if step == (N_PASS - 1) * N_PAIR + 1:
+                quantise_x()
+            if block == N_PASS - 1 and pair >= SECOND_LAG:
+                finish(pair - SECOND_LAG)
+
+        quantise_g(N_STEP - 1)
+        for pair in range(N_PAIR - SECOND_LAG, N_PAIR):
+            second_matmul(pair)
+            finish(pair)

@@ -21,7 +21,8 @@ N_PASS = SIZE // PASS
 PAIR = 256
 N_PAIR = SIZE // PAIR
 N_STEP = N_PASS * N_PAIR
-REGROUP_FROM = 3
+LOAD_BLOCK_1_AFTER = 3
+REGROUP_FROM = 2
 SECOND_LAG = 2
 
 GAMMA = 0.5
@@ -109,9 +110,9 @@ def tile_combinelayer_pa_kernel(tc, support0, f, support1, adj, x, h0, out):
             s1_scales[block] = keep.tile([P, N_PASS * PASS], U8, name="s1_scales%d" % block, align_bytes=64)
 
         def regroup_support1(block, c, on_vector):
-            rows = s1_rows[block][:].rearrange("q (c t w e) -> q c e w t", c=N_PASS, t=4, e=2)
+            rows = s1_rows[block][:].rearrange("q (c t w e) -> q c w e t", c=N_PASS, t=4, e=2)
             grouped = stage.tile([P, 4 * PASS], BF16, name="s1_grouped", tag="s1_grouped", bufs=3, align_bytes=64)
-            view = grouped[:].rearrange("q (e w t) -> q e w t", e=2, t=4)
+            view = grouped[:].rearrange("q (e w t) -> q w e t", e=2, t=4)
             if on_vector:
                 nc.vector.tensor_copy(out=view, in_=rows[:, c])
             else:
@@ -292,10 +293,8 @@ def tile_combinelayer_pa_kernel(tc, support0, f, support1, adj, x, h0, out):
         for pair in range(1, N_PAIR):
             load_support0(pair)
             load_adj(0, pair)
-            if pair == REGROUP_FROM:
+            if pair == LOAD_BLOCK_1_AFTER:
                 load_support1(1)
-        for pair in range(N_PAIR):
-            load_adj(1, pair)
 
         turn_and_scale_support0(0, 0)
         turn_and_scale_support0(0, 1)
@@ -311,6 +310,8 @@ def tile_combinelayer_pa_kernel(tc, support0, f, support1, adj, x, h0, out):
         turn_and_halve_adj(0)
 
         load_support1(2)
+        for pair in range(N_PAIR):
+            load_adj(1, pair)
         load_x_h0()
         for pair in range(N_PAIR):
             load_adj(2, pair)
@@ -336,13 +337,8 @@ def tile_combinelayer_pa_kernel(tc, support0, f, support1, adj, x, h0, out):
             if block == N_PASS - 1 and pair >= SECOND_LAG:
                 second_matmul(pair - SECOND_LAG)
 
-            regroup = None
-            if block == 0 and pair >= REGROUP_FROM:
-                regroup = pair - REGROUP_FROM
-            if block == 1 and pair < N_PASS:
-                regroup = pair
-            if regroup is not None:
-                regroup_support1(block + 1, regroup, False)
+            if REGROUP_FROM <= step < REGROUP_FROM + 2 * N_PASS:
+                regroup_support1(1 + (step - REGROUP_FROM) // N_PASS, (step - REGROUP_FROM) % N_PASS, False)
             if step == (N_PASS - 1) * N_PAIR:
                 regroup_x_scale_h0()
 
@@ -351,13 +347,9 @@ def tile_combinelayer_pa_kernel(tc, support0, f, support1, adj, x, h0, out):
                 quantise_a(pair + 1, 2)
             if step > 0:
                 quantise_g(step - 1)
-            if regroup is not None and regroup > 0:
-                quantise_support1(block + 1, regroup - 1)
-            if block == 1 and pair == N_PASS:
-                quantise_support1(block + 1, N_PASS - 1)
+            if REGROUP_FROM < step <= REGROUP_FROM + 2 * N_PASS:
+                quantise_support1(1 + (step - 1 - REGROUP_FROM) // N_PASS, (step - 1 - REGROUP_FROM) % N_PASS)
             blend(step, 1)
-            if block == 0 and pair == N_PAIR - 1:
-                quantise_support1(block + 1, N_PASS - 1)
             if step == (N_PASS - 1) * N_PAIR + 1:
                 quantise_x()
             if block == N_PASS - 1 and pair >= SECOND_LAG:

@@ -23,7 +23,7 @@ N_PAIR = SIZE // PAIR
 N_STEP = N_PASS * N_PAIR
 LOAD_BLOCK_1_AFTER = 3
 REGROUP_FROM = 2
-SECOND_LAG = 2
+SECOND_LAG = 4
 
 GAMMA = 0.5
 ALPHA = 0.1
@@ -38,8 +38,7 @@ def tile_combinelayer_pa_kernel(tc, support0, f, support1, adj, x, h0, out):
         keep = ctx.enter_context(tc.tile_pool(name="keep", bufs=1))
         stage = ctx.enter_context(tc.tile_pool(name="stage", bufs=4))
         turned = ctx.enter_context(tc.psum_pool(name="turned", bufs=4))
-        sums = ctx.enter_context(tc.psum_pool(name="sums", bufs=3))
-        result = ctx.enter_context(tc.psum_pool(name="result", bufs=1))
+        sums = ctx.enter_context(tc.psum_pool(name="sums", bufs=4))
 
         ident = const.tile([P, P], F32, name="ident")
         make_identity(nc, ident[:])
@@ -215,7 +214,7 @@ def tile_combinelayer_pa_kernel(tc, support0, f, support1, adj, x, h0, out):
         def blend(step, j):
             if j == 0:
                 g_grouped[step] = stage.tile(
-                    [P, 4 * PAIR], BF16, name="g_grouped", tag="g_grouped", bufs=3, align_bytes=64
+                    [P, 4 * PAIR], BF16, name="g_grouped", tag="g_grouped", bufs=N_PAIR + 1, align_bytes=64
                 )
             nc.vector.scalar_tensor_tensor(
                 out=g_grouped[step][:, j * 4 * P : (j + 1) * 4 * P],
@@ -257,7 +256,7 @@ def tile_combinelayer_pa_kernel(tc, support0, f, support1, adj, x, h0, out):
         hi_bank = {}
 
         def second_matmul(pair):
-            bank = result.tile([P, 2 * D], F32, name="hi_bank", tag="result")
+            bank = sums.tile([P, 2 * D], F32, name="hi_bank", tag="sums")
             for j in range(2):
                 for c in range(N_PASS):
                     cols = slice(c * PAIR + j * P, c * PAIR + (j + 1) * P)
@@ -273,7 +272,7 @@ def tile_combinelayer_pa_kernel(tc, support0, f, support1, adj, x, h0, out):
             hi_bank[pair] = bank
 
         def finish(pair):
-            rows = stage.tile([P, 2 * D], F32, name="out_rows", tag="out_rows", bufs=2)
+            rows = stage.tile([P, 2 * D], F32, name="out_rows", tag="out_rows", bufs=SECOND_LAG)
             nc.vector.scalar_tensor_tensor(
                 out=rows[:],
                 in0=hi_bank[pair][:],
@@ -345,8 +344,10 @@ def tile_combinelayer_pa_kernel(tc, support0, f, support1, adj, x, h0, out):
             blend(step, 0)
             if prepare:
                 quantise_a(pair + 1, 2)
-            if step > 0:
+            if step - 1 >= N_PAIR:
                 quantise_g(step - 1)
+            if block == 1:
+                quantise_g(step - N_PAIR)
             if REGROUP_FROM < step <= REGROUP_FROM + 2 * N_PASS:
                 quantise_support1(1 + (step - 1 - REGROUP_FROM) // N_PASS, (step - 1 - REGROUP_FROM) % N_PASS)
             blend(step, 1)
@@ -355,7 +356,9 @@ def tile_combinelayer_pa_kernel(tc, support0, f, support1, adj, x, h0, out):
             if block == N_PASS - 1 and pair >= SECOND_LAG:
                 finish(pair - SECOND_LAG)
 
-        quantise_g(N_STEP - 1)
-        for pair in range(N_PAIR - SECOND_LAG, N_PAIR):
+        for pair in range(N_PAIR - SECOND_LAG, N_PAIR - 1):
             second_matmul(pair)
+        quantise_g(N_STEP - 1)
+        second_matmul(N_PAIR - 1)
+        for pair in range(N_PAIR - SECOND_LAG, N_PAIR):
             finish(pair)

@@ -5,6 +5,7 @@ from concourse.masks import make_identity
 
 F32 = mybir.dt.float32
 BF16 = mybir.dt.bfloat16
+I32 = mybir.dt.int32
 U32 = mybir.dt.uint32
 U8 = mybir.dt.uint8
 FP8X4 = mybir.dt.float8_e4m3fn_x4
@@ -46,11 +47,13 @@ def tile_combinelayer_pa_kernel(tc, support0, f, support1, adj, x, h0, out):
         ctx.enter_context(tc.manual_schedule())
 
 
+        f_rows = const.tile([P, HALF], BF16, name="f_rows")
+        nc.vector.memset(f_rows[:].bitcast(I32), 0)
+        nc.scalar.dma_start(out=f_rows[0 : 2 * N_PASS, :], in_=f.rearrange("(h w) -> h w", w=HALF))
+        f_bank = turned.tile([P, 2 * PAIR], F32, name="f_bank", tag="turned")
+        nc.tensor.transpose(f_bank[:, 0:P], f_rows[:].bitcast(F32), ident[:])
         f_word = const.tile([P, N_PASS * 4], BF16, name="f_word")
-        nc.scalar.dma_start(
-            out=f_word[:].rearrange("q (h e) -> q h e", e=2),
-            in_=f.rearrange("(h q e) -> q h e", q=P, e=2),
-        )
+        nc.vector.tensor_copy(out=f_word[:].bitcast(F32), in_=f_bank[:, 0 : 2 * N_PASS])
         warm = const.tile([P, 1], F32, name="warm")
         nc.scalar.activation(out=warm[:], in_=ident[:, 0:1], func=COPY, scale=1.0)
 

from contextlib import ExitStack

import concourse.mybir as mybir
from concourse.masks import make_identity

F32 = mybir.dt.float32
BF16 = mybir.dt.bfloat16
I32 = mybir.dt.int32
U32 = mybir.dt.uint32
U8 = mybir.dt.uint8
FP8X4 = mybir.dt.float8_e4m3fn_x4
ADD = mybir.AluOpType.add
MULT = mybir.AluOpType.mult
COPY = mybir.ActivationFunctionType.Copy

P = 128
SIZE = 1536
D = 128
PASS = 512
HALF = 256
N_PASS = SIZE // PASS
PAIR = 256
N_PAIR = SIZE // PAIR
N_STEP = N_PASS * N_PAIR
LOAD_BLOCK_1_AFTER = 3
REGROUP_FROM = 2
SECOND_LAG = 4

GAMMA = 0.5
ALPHA = 0.1

FLOPS = 2 * SIZE * SIZE * SIZE + 2 * SIZE * SIZE * D


def tile_combinelayer_pa_kernel(tc, support0, f, support1, adj, x, h0, out):
    nc = tc.nc
    with ExitStack() as ctx:
        const = ctx.enter_context(tc.tile_pool(name="const", bufs=1))
        keep = ctx.enter_context(tc.tile_pool(name="keep", bufs=1))
        stage = ctx.enter_context(tc.tile_pool(name="stage", bufs=4))
        turned = ctx.enter_context(tc.psum_pool(name="turned", bufs=4))
        sums = ctx.enter_context(tc.psum_pool(name="sums", bufs=4))

        ident = const.tile([P, P], F32, name="ident")
        make_identity(nc, ident[:])

        ctx.enter_context(tc.manual_schedule())


        f_rows = const.tile([P, HALF], BF16, name="f_rows")
        nc.vector.memset(f_rows[:].bitcast(I32), 0)
        nc.scalar.dma_start(out=f_rows[0 : 2 * N_PASS, :], in_=f.rearrange("(h w) -> h w", w=HALF))
        f_bank = turned.tile([P, 2 * PAIR], F32, name="f_bank", tag="turned")
        nc.tensor.transpose(f_bank[:, 0:P], f_rows[:].bitcast(F32), ident[:])
        f_word = const.tile([P, N_PASS * 4], BF16, name="f_word")
        nc.vector.tensor_copy(out=f_word[:].bitcast(F32), in_=f_bank[:, 0 : 2 * N_PASS])
        warm = const.tile([P, 1], F32, name="warm")
        nc.scalar.activation(out=warm[:], in_=ident[:, 0:1], func=COPY, scale=1.0)

        s0_rows = {}
        s1_rows = {}
        adj_rows = {}

        def load_support0(pair):
            rows = keep.tile([P, 2 * SIZE], BF16, name="s0_rows%d" % pair)
            nc.sync.dma_start(
                out=rows[:].rearrange("p (j k) -> p j k", j=2),
                in_=support0[pair * PAIR : (pair + 1) * PAIR, :].rearrange("(j p) k -> p j k", p=P),
            )
            s0_rows[pair] = rows

        def load_support1(block):
            rows = keep.tile([P, N_PASS * 4 * PASS], BF16, name="s1_rows", tag="s1_rows", bufs=2)
            view = rows[:].rearrange("q (h e n) -> q h e n", e=2, n=PASS)
            for h in range(2 * N_PASS):
                nc.sync.dma_start(
                    out=view[:, h, :, :],
                    in_=support1[
                        h * HALF : (h + 1) * HALF, block * PASS : (block + 1) * PASS
                    ].rearrange("(q e) n -> q e n", e=2),
                )
            s1_rows[block] = rows

        def load_adj(block, pair):
            rows = keep.tile([P, 2 * PASS], BF16, name="adj_rows%d_%d" % (block, pair))
            nc.sync.dma_start(
                out=rows[:].rearrange("p (j n) -> p j n", j=2),
                in_=adj[
                    pair * PAIR : (pair + 1) * PAIR, block * PASS : (block + 1) * PASS
                ].rearrange("(j p) n -> p j n", p=P),
            )
            adj_rows[(block, pair)] = rows

        x_rows = keep.tile([P, N_PASS * 4 * D], BF16, name="x_rows")
        h0_rows = keep.tile([P, (SIZE // P) * D], BF16, name="h0_rows")

        def load_x_h0():
            nc.sync.dma_start(
                out=x_rows[:].rearrange("q (h e d) -> q h e d", e=2, d=D),
                in_=x.rearrange("(h q e) d -> q h e d", q=P, e=2),
            )
            nc.sync.dma_start(
                out=h0_rows[:].rearrange("p (j d) -> p j d", d=D),
                in_=h0.rearrange("(j p) d -> p j d", p=P),
            )

        s1_codes = {}
        s1_scales = {}
        s1_grouped = {}
        for block in range(N_PASS):
            s1_codes[block] = keep.tile([P, N_PASS * PASS], U32, name="s1_codes%d" % block, align_bytes=64)
            s1_scales[block] = keep.tile([P, N_PASS * PASS], U8, name="s1_scales%d" % block, align_bytes=64)

        def regroup_support1(block, c, on_vector):
            rows = s1_rows[block][:].rearrange("q (c t w e) -> q c w e t", c=N_PASS, t=4, e=2)
            grouped = stage.tile([P, 4 * PASS], BF16, name="s1_grouped", tag="s1_grouped", bufs=3, align_bytes=64)
            view = grouped[:].rearrange("q (e w t) -> q w e t", e=2, t=4)
            if on_vector:
                nc.vector.tensor_copy(out=view, in_=rows[:, c])
            else:
                nc.scalar.copy(out=view, in_=rows[:, c])
            s1_grouped[(block, c)] = grouped

        def quantise_support1(block, c):
            nc.vector.quantize_mx(
                out=s1_codes[block][:, c * PASS : (c + 1) * PASS].bitcast(FP8X4),
                scales=s1_scales[block][:, c * PASS : (c + 1) * PASS],
                in_=s1_grouped[(block, c)][:],
            )

        a_codes = {}
        a_scales = {}
        a_grouped = {}
        for pair in range(N_PAIR):
            a_codes[pair] = keep.tile([P, N_PASS * PAIR], U32, name="a_codes%d" % pair, align_bytes=64)
            a_scales[pair] = keep.tile([P, N_PASS * PAIR], U8, name="a_scales%d" % pair, align_bytes=64)

        def turn_and_scale_support0(pair, c):
            words = s0_rows[pair][:].bitcast(F32).rearrange("p (j w) -> p j w", j=2)
            bank = turned.tile([P, 2 * PAIR], F32, name="a_bank", tag="turned")
            for u in range(2):
                for j in range(2):
                    nc.tensor.transpose(
                        bank[:, u * PAIR + j * P : u * PAIR + (j + 1) * P],
                        words[:, j, (2 * c + u) * P : (2 * c + u + 1) * P],
                        ident[:],
                    )
            grouped = stage.tile([P, 4 * PAIR], BF16, name="a_grouped", tag="a_grouped", align_bytes=64)
            nc.vector.tensor_tensor(
                out=grouped[:].rearrange("q (m u e) -> q m u e", u=2, e=2),
                in0=bank[:].bitcast(BF16).rearrange("q (u m e) -> q m u e", u=2, e=2),
                in1=f_word[:, 4 * c : 4 * c + 4]
                .rearrange("q (u e) -> q u e", e=2)
                .unsqueeze(1)
                .to_broadcast([P, PAIR, 2, 2]),
                op=MULT,
            )
            a_grouped[(pair, c)] = grouped

        def quantise_a(pair, c):
            nc.vector.quantize_mx(
                out=a_codes[pair][:, c * PAIR : (c + 1) * PAIR].bitcast(FP8X4),
                scales=a_scales[pair][:, c * PAIR : (c + 1) * PAIR],
                in_=a_grouped[(pair, c)][:],
            )

        adj_half = {}

        def turn_and_halve_adj(step):
            block, pair = divmod(step, N_PAIR)
            words = adj_rows[(block, pair)][:].bitcast(F32).rearrange("p (j w) -> p j w", j=2)
            bank = turned.tile([P, 2 * PAIR], F32, name="adj_bank", tag="turned")
            for u in range(2):
                for j in range(2):
                    nc.tensor.transpose(
                        bank[:, u * PAIR + j * P : u * PAIR + (j + 1) * P],
                        words[:, j, u * P : (u + 1) * P],
                        ident[:],
                    )
            half = stage.tile([P, 4 * PAIR], BF16, name="adj_half", tag="adj_half")
            nc.scalar.activation(
                out=half[:].rearrange("q (m u e) -> q m u e", u=2, e=2),
                in_=bank[:].bitcast(BF16).rearrange("q (u m e) -> q m u e", u=2, e=2),
                func=COPY,
                scale=1.0 - GAMMA,
            )
            adj_half[step] = half

        g_codes = {}
        g_scales = {}
        g_grouped = {}
        p_bank = {}
        for pair in range(N_PAIR):
            g_codes[pair] = keep.tile([P, N_PASS * PAIR], U32, name="g_codes%d" % pair, align_bytes=64)
            g_scales[pair] = keep.tile([P, N_PASS * PAIR], U8, name="g_scales%d" % pair, align_bytes=64)

        def first_matmul(step, j):
            block, pair = divmod(step, N_PAIR)
            bank = sums.tile([P, 4 * P], F32, name="p_bank", tag="sums")
            for u in range(2):
                for e in range(2):
                    t = 2 * u + e
                    for c in range(N_PASS):
                        cols = slice(c * PASS + e * HALF + u * P, c * PASS + e * HALF + (u + 1) * P)
                        rows = slice(c * PAIR + j * P, c * PAIR + (j + 1) * P)
                        nc.tensor.matmul_mx(
                            out=bank[:, t * P : (t + 1) * P],
                            lhsT=s1_codes[block][:, cols].bitcast(FP8X4),
                            lhsT_scale=s1_scales[block][:, cols],
                            rhs=a_codes[pair][:, rows].bitcast(FP8X4),
                            rhs_scale=a_scales[pair][:, rows],
                            start=(c == 0),
                            stop=(c == N_PASS - 1),
                        )
            p_bank[(step, j)] = bank

        def blend(step, j):
            if j == 0:
                g_grouped[step] = stage.tile(
                    [P, 4 * PAIR], BF16, name="g_grouped", tag="g_grouped", bufs=N_PAIR + 1, align_bytes=64
                )
            nc.vector.scalar_tensor_tensor(
                out=g_grouped[step][:, j * 4 * P : (j + 1) * 4 * P],
                in0=p_bank[(step, j)][:].rearrange("q (t m) -> q m t", t=4),
                scalar=GAMMA,
                in1=adj_half[step][:, j * 4 * P : (j + 1) * 4 * P],
                op0=MULT,
                op1=ADD,
            )

        def quantise_g(step):
            block, pair = divmod(step, N_PAIR)
            nc.vector.quantize_mx(
                out=g_codes[pair][:, block * PAIR : (block + 1) * PAIR].bitcast(FP8X4),
                scales=g_scales[pair][:, block * PAIR : (block + 1) * PAIR],
                in_=g_grouped[step][:],
            )

        x_codes = keep.tile([P, N_PASS * D], U32, name="x_codes", align_bytes=64)
        x_scales = keep.tile([P, N_PASS * D], U8, name="x_scales", align_bytes=64)
        x_grouped = keep.tile([P, N_PASS * 4 * D], BF16, name="x_grouped", align_bytes=64)
        h0_part = keep.tile([P, (SIZE // P) * D], F32, name="h0_part")

        def regroup_x_scale_h0():
            nc.scalar.copy(
                out=x_grouped[:].rearrange("q (c d t) -> q c d t", c=N_PASS, t=4),
                in_=x_rows[:].rearrange("q (c t d) -> q c d t", c=N_PASS, t=4),
            )
            nc.scalar.activation(out=h0_part[:], in_=h0_rows[:], func=COPY, scale=ALPHA)

        def quantise_x():
            for c in range(N_PASS):
                nc.vector.quantize_mx(
                    out=x_codes[:, c * D : (c + 1) * D].bitcast(FP8X4),
                    scales=x_scales[:, c * D : (c + 1) * D],
                    in_=x_grouped[:, c * 4 * D : (c + 1) * 4 * D],
                )

        hi_bank = {}

        def second_matmul(pair):
            bank = sums.tile([P, 2 * D], F32, name="hi_bank", tag="sums")
            for j in range(2):
                for c in range(N_PASS):
                    cols = slice(c * PAIR + j * P, c * PAIR + (j + 1) * P)
                    nc.tensor.matmul_mx(
                        out=bank[:, j * D : (j + 1) * D],
                        lhsT=g_codes[pair][:, cols].bitcast(FP8X4),
                        lhsT_scale=g_scales[pair][:, cols],
                        rhs=x_codes[:, c * D : (c + 1) * D].bitcast(FP8X4),
                        rhs_scale=x_scales[:, c * D : (c + 1) * D],
                        start=(c == 0),
                        stop=(c == N_PASS - 1),
                    )
            hi_bank[pair] = bank

        def finish(pair):
            rows = stage.tile([P, 2 * D], F32, name="out_rows", tag="out_rows", bufs=SECOND_LAG)
            nc.vector.scalar_tensor_tensor(
                out=rows[:],
                in0=hi_bank[pair][:],
                scalar=1.0 - ALPHA,
                in1=h0_part[:, pair * 2 * D : (pair + 1) * 2 * D],
                op0=MULT,
                op1=ADD,
            )
            nc.sync.dma_start(
                out=out[pair * PAIR : (pair + 1) * PAIR, :].rearrange("(j p) d -> p j d", p=P),
                in_=rows[:].rearrange("p (j d) -> p j d", d=D),
            )

        load_support0(0)
        load_support1(0)
        load_adj(0, 0)
        for pair in range(1, N_PAIR):
            load_support0(pair)
            load_adj(0, pair)
            if pair == LOAD_BLOCK_1_AFTER:
                load_support1(1)

        turn_and_scale_support0(0, 0)
        turn_and_scale_support0(0, 1)
        quantise_a(0, 0)
        turn_and_scale_support0(0, 2)
        quantise_a(0, 1)
        regroup_support1(0, 0, False)
        regroup_support1(0, 1, False)
        quantise_a(0, 2)
        regroup_support1(0, 2, True)
        for c in range(N_PASS):
            quantise_support1(0, c)
        turn_and_halve_adj(0)

        load_support1(2)
        for pair in range(N_PAIR):
            load_adj(1, pair)
        load_x_h0()
        for pair in range(N_PAIR):
            load_adj(2, pair)

        for step in range(N_STEP):
            block, pair = divmod(step, N_PAIR)
            prepare = block == 0 and pair + 1 < N_PAIR

            if prepare:
                turn_and_scale_support0(pair + 1, 0)
                turn_and_scale_support0(pair + 1, 1)
                quantise_a(pair + 1, 0)
                turn_and_scale_support0(pair + 1, 2)
                quantise_a(pair + 1, 1)
            if block == 0:
                turn_and_halve_adj(step + 1)
            elif step % 2 == 0:
                for later in (step + 1, step + 2):
                    if later < N_STEP:
                        turn_and_halve_adj(later)
            first_matmul(step, 0)
            first_matmul(step, 1)
            if block == N_PASS - 1 and pair >= SECOND_LAG:
                second_matmul(pair - SECOND_LAG)

            if REGROUP_FROM <= step < REGROUP_FROM + 2 * N_PASS:
                regroup_support1(1 + (step - REGROUP_FROM) // N_PASS, (step - REGROUP_FROM) % N_PASS, False)
            if step == (N_PASS - 1) * N_PAIR:
                regroup_x_scale_h0()

            blend(step, 0)
            if prepare:
                quantise_a(pair + 1, 2)
            if step - 1 >= N_PAIR:
                quantise_g(step - 1)
            if block == 1:
                quantise_g(step - N_PAIR)
            if REGROUP_FROM < step <= REGROUP_FROM + 2 * N_PASS:
                quantise_support1(1 + (step - 1 - REGROUP_FROM) // N_PASS, (step - 1 - REGROUP_FROM) % N_PASS)
            blend(step, 1)
            if step == (N_PASS - 1) * N_PAIR + 1:
                quantise_x()
            if block == N_PASS - 1 and pair >= SECOND_LAG:
                finish(pair - SECOND_LAG)

        for pair in range(N_PAIR - SECOND_LAG, N_PAIR - 1):
            second_matmul(pair)
        quantise_g(N_STEP - 1)
        second_matmul(N_PAIR - 1)
        for pair in range(N_PAIR - SECOND_LAG, N_PAIR):
            finish(pair)
